import numpy as np
import ml_dtypes


def mxq(x, axis, fmt="e4m3"):
    dtype, down = {"e4m3": (ml_dtypes.float8_e4m3fn, 7), "e5m2": (ml_dtypes.float8_e5m2, 14)}[fmt]
    v = np.moveaxis(np.asarray(x, np.float32).astype(ml_dtypes.bfloat16).astype(np.float64), axis, -1)
    blocks = v.reshape(v.shape[:-1] + (-1, 32))
    amax = np.abs(blocks).max(-1, keepdims=True)
    byte = np.maximum(np.where(amax > 0, np.frexp(amax)[1] - 1 + 127, 0) - down, 1)
    scale = np.exp2(byte - 127.0)
    codes = (blocks / scale).astype(np.float32).astype(dtype).astype(np.float64)
    return np.moveaxis((codes * scale).reshape(v.shape), -1, axis)


WIDE = False


def mx_kscale(k):
    if not WIDE:
        return np.ones(k)
    levels = np.array([10, -10, 5, -5, 0])
    a = np.random.permutation(np.resize(levels, k // 512 * 4)).reshape(k // 512, 4)
    idx = np.arange(k)
    return np.exp2(a[idx // 512, idx % 128 // 32])


BF16 = ml_dtypes.bfloat16


def bf(x):
    return np.asarray(x, np.float32).astype(BF16)


def f64(x):
    return np.asarray(x).astype(np.float64)


E2M1 = np.array([0.0, 0.5, 1.0, 1.5, 2.0, 3.0, 4.0, 6.0, -0.0, -0.5, -1.0, -1.5, -2.0, -3.0, -4.0, -6.0])


def pack_weight(w, fmt):
    k, n = w.shape
    w = f64(bf(w)).reshape(k // 32, 32, n)
    amax = np.abs(w).max(1)
    if fmt == "e4m3":
        byte = np.frexp(amax)[1] - 1 + 127 - 7
    else:
        mant, ex = np.frexp(amax / 6.0)
        byte = np.where(mant > 0.5, ex, ex - 1) + 127
    byte = np.clip(np.where(amax > 0, byte, 1), 1, 254)
    scaled = (w * np.exp2(127.0 - byte)[:, None, :]).reshape(k, n).astype(np.float32)
    by_word = np.ascontiguousarray(scaled.reshape(k // 512, 128, 4, n).transpose(0, 1, 3, 2))
    if fmt == "e4m3":
        words = by_word.astype(ml_dtypes.float8_e4m3fn).view(np.uint8)
    else:
        c = by_word.astype(ml_dtypes.float4_e2m1fn).view(np.uint8) & 0xF
        words = c[..., 0::2] | (c[..., 1::2] << 4)
    return np.ascontiguousarray(words), np.ascontiguousarray(byte.astype(np.uint8).reshape(k // 512, 16, n))


def unpack_weight(words, scales, fmt):
    g, p, n, _ = words.shape
    if fmt == "e4m3":
        vals = np.ascontiguousarray(words).view(ml_dtypes.float8_e4m3fn).astype(np.float64)
    else:
        nib = np.empty((g, p, n, 4), np.uint8)
        nib[..., 0::2] = words & 0xF
        nib[..., 1::2] = words >> 4
        vals = E2M1[nib]
    vals = vals * np.repeat(np.exp2(scales.astype(np.float64) - 127.0), 8, axis=1)[..., None]
    return vals.transpose(0, 1, 3, 2).reshape(g * 512, n)


def pack4(w):
    words, scales = pack_weight(w, "e2m1")
    return words.reshape(words.shape[0], 128, -1), scales


def unpack4(words, scales):
    return unpack_weight(words.reshape(words.shape[0], 128, -1, 2), scales, "e2m1")


B, S, IN, OUT = 2, 128, 2048, 5632


def setup_inputs():
    s = mx_kscale(IN)
    x = bf(np.random.standard_normal((B, S, IN)) * s)
    w = np.random.standard_normal((IN, OUT)) * 0.022 / s[:, None]
    w_words, w_scales = pack4(w)
    return {"x": x, "w_words": w_words, "w_scales": w_scales}


def reference(x, w_words, w_scales):
    w = unpack4(w_words, w_scales)
    in_f, out_f = w.shape
    x = f64(x)
    out_shape = x.shape[:-1] + (out_f,)
    x2 = x.reshape(-1, in_f)
    out = mxq(x2, 1, "e4m3") @ w
    return out.reshape(out_shape)

@@ -1,0 +1,144 @@
+from contextlib import ExitStack
+
+import concourse.mybir as mybir
+from concourse.masks import make_identity
+
+F32 = mybir.dt.float32
+BF16 = mybir.dt.bfloat16
+I32 = mybir.dt.int32
+U8 = mybir.dt.uint8
+U32 = mybir.dt.uint32
+FP8X4 = mybir.dt.float8_e4m3fn_x4
+FP4X4 = mybir.dt.float4_e2m1fn_x4
+
+P = 128
+ROW_TILES = 2
+PASSES = 4
+N_TILE = 512
+COL_TILES = 11
+FLOPS = 2 * 256 * 2048 * 5632
+
+WORD_CHUNKS = ((0, 1), (1, 1), (2, 2), (4, 3), (7, 4))
+PLANE_GROUPS = ((0, 2), (2, 4), (6, 5))
+STORE_GROUPS = ((0, 2), (2, 2), (4, 2), (6, 2), (8, 2), (10, 1))
+
+
+def find(groups, j):
+    for idx, (first, count) in enumerate(groups):
+        if first <= j < first + count:
+            return idx, j - first
+    raise ValueError("column tile outside the groups")
+
+
+def tile_quantlinear_kernel(tc, x, w_words, w_scales, out):
+    nc = tc.nc
+    words_dram = w_words.bitcast(I32).rearrange("g p b -> p g b")
+    scales_i32 = w_scales.bitcast(I32).rearrange("g q b -> q g b")
+    scales_f32 = w_scales.bitcast(F32).rearrange("g q b -> q g b")
+
+    with ExitStack() as ctx:
+        keep = ctx.enter_context(tc.tile_pool(name="keep", bufs=1))
+        psum = ctx.enter_context(tc.psum_pool(name="psum", bufs=8))
+        ctx.enter_context(tc.manual_schedule())
+
+        ident = keep.tile([P, P], F32, name="ident")
+        order = keep.tile([P, 8], F32, name="order")
+        x_raw = [keep.tile([P, 2048], BF16, name="x_raw%d" % m) for m in range(ROW_TILES)]
+        grouped = [
+            keep.tile([P, 2, P, 4], BF16, name="grouped%d" % i, align_bytes=64) for i in range(2 * ROW_TILES)
+        ]
+        x_codes = [keep.tile([P, 2 * P], U32, name="x_codes%d" % i, align_bytes=64) for i in range(2 * ROW_TILES)]
+        x_plane = [keep.tile([P, 2 * P], U8, name="x_plane%d" % i, align_bytes=64) for i in range(2 * ROW_TILES)]
+        w_chunk = [
+            keep.tile([P, PASSES, 2 * N_TILE * count], U8, name="w_chunk%d" % c, align_bytes=64)
+            for c, (first, count) in enumerate(WORD_CHUNKS)
+        ]
+        w_plane = [
+            keep.tile([P, PASSES, N_TILE * count], U8, name="w_plane%d" % s, align_bytes=64)
+            for s, (first, count) in enumerate(PLANE_GROUPS)
+        ]
+        staged = [
+            [keep.tile([P, N_TILE * count], F32, name="staged%d_%d" % (m, t)) for t, (first, count) in enumerate(STORE_GROUPS)]
+            for m in range(ROW_TILES)
+        ]
+
+        def zero_planes(s):
+            nc.vector.memset(w_plane[s][:].bitcast(I32), 0)
+
+        def load_planes(s, software_queue):
+            first, count = PLANE_GROUPS[s]
+            cols = slice(first * N_TILE // 4, (first + count) * N_TILE // 4)
+            for r in range(4):
+                if software_queue:
+                    nc.gpsimd.dma_start(out=w_plane[s][:].bitcast(F32)[r:P:32, :, :], in_=scales_f32[r:16:4, :, cols])
+                else:
+                    nc.sync.dma_start(out=w_plane[s][:].bitcast(I32)[r:P:32, :, :], in_=scales_i32[r:16:4, :, cols])
+
+        def load_words(c):
+            first, count = WORD_CHUNKS[c]
+            cols = slice(first * N_TILE // 2, (first + count) * N_TILE // 2)
+            nc.sync.dma_start(out=w_chunk[c][:].bitcast(I32), in_=words_dram[:, :, cols])
+
+        make_identity(nc, ident[:])
+        for m in range(ROW_TILES):
+            nc.sync.dma_start(out=x_raw[m][:], in_=x[m])
+        zero_planes(0)
+        nc.vector.tensor_copy(out=order[:, 0:1], in_=ident[:, 0:1])
+        zero_planes(1)
+        load_planes(0, False)
+        for c in range(len(WORD_CHUNKS)):
+            load_words(c)
+        load_planes(1, True)
+
+        banks = []
+        for m in range(ROW_TILES):
+            x_words = x_raw[m][:].bitcast(F32)
+            for g in range(PASSES):
+                xt = psum.tile([P, 2, P], F32, name="xt%d_%d" % (m, g), tag="bank")
+                for u in range(2):
+                    nc.tensor.transpose(xt[:, u, :], x_words[:, 256 * g + u : 256 * (g + 1) : 2], ident[:])
+                banks.append(xt)
+        for m in range(ROW_TILES):
+            for h in range(2):
+                view = grouped[2 * m + h][:].bitcast(F32)
+                nc.vector.tensor_copy(out=view[:, 0], in_=banks[4 * m + 2 * h][:].rearrange("p u r -> p r u"))
+                nc.scalar.copy(out=view[:, 1], in_=banks[4 * m + 2 * h + 1][:].rearrange("p u r -> p r u"))
+            for h in range(2):
+                i = 2 * m + h
+                nc.vector.quantize_mx(
+                    out=x_codes[i][:].bitcast(FP8X4),
+                    scales=x_plane[i][:],
+                    in_=grouped[i][:].rearrange("p g r t -> p (g r t)"),
+                )
+        zero_planes(2)
+        load_planes(2, True)
+
+        for j in range(COL_TILES):
+            c, ci = find(WORD_CHUNKS, j)
+            s, si = find(PLANE_GROUPS, j)
+            t, ti = find(STORE_GROUPS, j)
+            for m in range(ROW_TILES):
+                acc = psum.tile([P, N_TILE], F32, name="acc%d_%d" % (m, j), tag="bank")
+                for g in range(PASSES):
+                    i = 2 * m + g // 2
+                    tok = slice(P * (g % 2), P * (g % 2 + 1))
+                    nc.tensor.matmul_mx(
+                        out=acc[:],
+                        lhsT=x_codes[i][:, tok].bitcast(FP8X4),
+                        lhsT_scale=x_plane[i][:, tok],
+                        rhs=w_chunk[c][:, g, 2 * N_TILE * ci : 2 * N_TILE * (ci + 1)].bitcast(FP4X4),
+                        rhs_scale=w_plane[s][:, g, N_TILE * si : N_TILE * (si + 1)],
+                        start=(g == 0),
+                        stop=(g == PASSES - 1),
+                    )
+                dst = staged[m][t][:, N_TILE * ti : N_TILE * (ti + 1)]
+                if m == 0:
+                    nc.vector.tensor_copy(out=dst, in_=acc[:])
+                else:
+                    nc.scalar.copy(out=dst, in_=acc[:])
+            first, count = STORE_GROUPS[t]
+            if ti == count - 1:
+                for m in range(ROW_TILES):
+                    nc.sync.dma_start(
+                        out=out[m, :, first * N_TILE : (first + count) * N_TILE], in_=staged[m][t][:]
+                    )

@@ -18,8 +18,9 @@ N_TILE = 512
 COL_TILES = 11
 FLOPS = 2 * 256 * 2048 * 5632
 
-WORD_CHUNKS = ((0, 1), (1, 1), (2, 2), (4, 3), (7, 4))
-PLANE_GROUPS = ((0, 2), (2, 4), (6, 5))
+WORD_CHUNKS = ((1, 1), (2, 2), (4, 2), (6, 2), (8, 2), (10, 1))
+PLANE_GROUPS = ((0, 2), (2, 3), (5, 3), (8, 3))
+GATE_AFTER_TILE = ((2, 0), (3, 3))
 STORE_GROUPS = ((0, 2), (2, 2), (4, 2), (6, 2), (8, 2), (10, 1))
 
 
@@ -49,6 +50,7 @@ def tile_quantlinear_kernel(tc, x, w_words, w_scales, out):
         ]
         x_codes = [keep.tile([P, 2 * P], U32, name="x_codes%d" % i, align_bytes=64) for i in range(2 * ROW_TILES)]
         x_plane = [keep.tile([P, 2 * P], U8, name="x_plane%d" % i, align_bytes=64) for i in range(2 * ROW_TILES)]
+        w_first = [keep.tile([P, 2 * N_TILE], U8, name="w_first%d" % g, align_bytes=64) for g in range(PASSES)]
         w_chunk = [
             keep.tile([P, PASSES, 2 * N_TILE * count], U8, name="w_chunk%d" % c, align_bytes=64)
             for c, (first, count) in enumerate(WORD_CHUNKS)
@@ -74,21 +76,23 @@ def tile_quantlinear_kernel(tc, x, w_words, w_scales, out):
                 else:
                     nc.sync.dma_start(out=w_plane[s][:].bitcast(I32)[r:P:32, :, :], in_=scales_i32[r:16:4, :, cols])
 
-        def load_words(c):
-            first, count = WORD_CHUNKS[c]
-            cols = slice(first * N_TILE // 2, (first + count) * N_TILE // 2)
-            nc.sync.dma_start(out=w_chunk[c][:].bitcast(I32), in_=words_dram[:, :, cols])
+        def let_go(s):
+            nc.vector.memset(w_plane[s][:].bitcast(I32)[:, 0, 0:1], 0)
+            load_planes(s, True)
 
         make_identity(nc, ident[:])
         for m in range(ROW_TILES):
             nc.sync.dma_start(out=x_raw[m][:], in_=x[m])
         zero_planes(0)
         nc.vector.tensor_copy(out=order[:, 0:1], in_=ident[:, 0:1])
-        zero_planes(1)
+        for s in range(1, len(PLANE_GROUPS)):
+            zero_planes(s)
         load_planes(0, False)
-        for c in range(len(WORD_CHUNKS)):
-            load_words(c)
-        load_planes(1, True)
+        for g in range(PASSES):
+            nc.sync.dma_start(out=w_first[g][:].bitcast(I32), in_=words_dram[:, g, 0 : N_TILE // 2])
+        for c, (first, count) in enumerate(WORD_CHUNKS):
+            cols = slice(first * N_TILE // 2, (first + count) * N_TILE // 2)
+            nc.sync.dma_start(out=w_chunk[c][:].bitcast(I32), in_=words_dram[:, :, cols])
 
         banks = []
         for m in range(ROW_TILES):
@@ -103,6 +107,8 @@ def tile_quantlinear_kernel(tc, x, w_words, w_scales, out):
                 view = grouped[2 * m + h][:].bitcast(F32)
                 nc.vector.tensor_copy(out=view[:, 0], in_=banks[4 * m + 2 * h][:].rearrange("p u r -> p r u"))
                 nc.scalar.copy(out=view[:, 1], in_=banks[4 * m + 2 * h + 1][:].rearrange("p u r -> p r u"))
+            if m == 0:
+                let_go(1)
             for h in range(2):
                 i = 2 * m + h
                 nc.vector.quantize_mx(
@@ -110,11 +116,8 @@ def tile_quantlinear_kernel(tc, x, w_words, w_scales, out):
                     scales=x_plane[i][:],
                     in_=grouped[i][:].rearrange("p g r t -> p (g r t)"),
                 )
-        zero_planes(2)
-        load_planes(2, True)
 
         for j in range(COL_TILES):
-            c, ci = find(WORD_CHUNKS, j)
             s, si = find(PLANE_GROUPS, j)
             t, ti = find(STORE_GROUPS, j)
             for m in range(ROW_TILES):
@@ -122,11 +125,16 @@ def tile_quantlinear_kernel(tc, x, w_words, w_scales, out):
                 for g in range(PASSES):
                     i = 2 * m + g // 2
                     tok = slice(P * (g % 2), P * (g % 2 + 1))
+                    if j == 0:
+                        words = w_first[g][:]
+                    else:
+                        c, ci = find(WORD_CHUNKS, j)
+                        words = w_chunk[c][:, g, 2 * N_TILE * ci : 2 * N_TILE * (ci + 1)]
                     nc.tensor.matmul_mx(
                         out=acc[:],
                         lhsT=x_codes[i][:, tok].bitcast(FP8X4),
                         lhsT_scale=x_plane[i][:, tok],
-                        rhs=w_chunk[c][:, g, 2 * N_TILE * ci : 2 * N_TILE * (ci + 1)].bitcast(FP4X4),
+                        rhs=words.bitcast(FP4X4),
                         rhs_scale=w_plane[s][:, g, N_TILE * si : N_TILE * (si + 1)],
                         start=(g == 0),
                         stop=(g == PASSES - 1),
@@ -134,6 +142,9 @@ def tile_quantlinear_kernel(tc, x, w_words, w_scales, out):
                 dst = staged[m][t][:, N_TILE * ti : N_TILE * (ti + 1)]
                 if m == 0:
                     nc.vector.tensor_copy(out=dst, in_=acc[:])
+                    for s_late, gate_tile in GATE_AFTER_TILE:
+                        if gate_tile == j:
+                            let_go(s_late)
                 else:
                     nc.scalar.copy(out=dst, in_=acc[:])
             first, count = STORE_GROUPS[t]

@@ -18,10 +18,10 @@ N_TILE = 512
 COL_TILES = 11
 FLOPS = 2 * 256 * 2048 * 5632
 
-WORD_CHUNKS = ((1, 1), (2, 2), (4, 2), (6, 2), (8, 2), (10, 1))
-PLANE_GROUPS = ((0, 2), (2, 3), (5, 3), (8, 3))
-GATE_AFTER_TILE = ((2, 0), (3, 3))
-STORE_GROUPS = ((0, 2), (2, 2), (4, 2), (6, 2), (8, 2), (10, 1))
+WORD_CHUNKS = ((1, 2), (3, 2), (5, 2), (7, 4))
+PLANE_GROUPS = ((0, 3), (3, 3), (6, 3), (9, 2))
+GATE_AFTER_TILE = ((2, 2), (3, 5))
+STORE_GROUPS = ((0, 3), (3, 3), (6, 2), (8, 2), (10, 1))
 
 
 def find(groups, j):
@@ -70,11 +70,16 @@ def tile_quantlinear_kernel(tc, x, w_words, w_scales, out):
         def load_planes(s, software_queue):
             first, count = PLANE_GROUPS[s]
             cols = slice(first * N_TILE // 4, (first + count) * N_TILE // 4)
-            for r in range(4):
-                if software_queue:
+            if software_queue:
+                for r in range(4):
                     nc.gpsimd.dma_start(out=w_plane[s][:].bitcast(F32)[r:P:32, :, :], in_=scales_f32[r:16:4, :, cols])
-                else:
-                    nc.sync.dma_start(out=w_plane[s][:].bitcast(I32)[r:P:32, :, :], in_=scales_i32[r:16:4, :, cols])
+            else:
+                for b in range(2):
+                    for r in range(4):
+                        nc.sync.dma_start(
+                            out=w_plane[s][:].bitcast(I32)[32 * b + r : P : 64, :, :],
+                            in_=scales_i32[4 * b + r : 16 : 8, :, cols],
+                        )
 
         def let_go(s):
             nc.vector.memset(w_plane[s][:].bitcast(I32)[:, 0, 0:1], 0)
@@ -91,6 +96,8 @@ def tile_quantlinear_kernel(tc, x, w_words, w_scales, out):
         for g in range(PASSES):
             nc.sync.dma_start(out=w_first[g][:].bitcast(I32), in_=words_dram[:, g, 0 : N_TILE // 2])
         for c, (first, count) in enumerate(WORD_CHUNKS):
+            if c == 1:
+                load_planes(1, False)
             cols = slice(first * N_TILE // 2, (first + count) * N_TILE // 2)
             nc.sync.dma_start(out=w_chunk[c][:].bitcast(I32), in_=words_dram[:, :, cols])
 
@@ -107,8 +114,6 @@ def tile_quantlinear_kernel(tc, x, w_words, w_scales, out):
                 view = grouped[2 * m + h][:].bitcast(F32)
                 nc.vector.tensor_copy(out=view[:, 0], in_=banks[4 * m + 2 * h][:].rearrange("p u r -> p r u"))
                 nc.scalar.copy(out=view[:, 1], in_=banks[4 * m + 2 * h + 1][:].rearrange("p u r -> p r u"))
-            if m == 0:
-                let_go(1)
             for h in range(2):
                 i = 2 * m + h
                 nc.vector.quantize_mx(

@@ -22,6 +22,7 @@ WORD_CHUNKS = ((1, 2), (3, 2), (5, 2), (7, 4))
 PLANE_GROUPS = ((0, 3), (3, 3), (6, 3), (9, 2))
 GATE_AFTER_TILE = ((2, 2), (3, 5))
 STORE_GROUPS = ((0, 3), (3, 3), (6, 2), (8, 2), (10, 1))
+IDLE_MATMULS = (7, 2, 2)
 
 
 def find(groups, j):
@@ -39,8 +40,16 @@ def tile_quantlinear_kernel(tc, x, w_words, w_scales, out):
 
     with ExitStack() as ctx:
         keep = ctx.enter_context(tc.tile_pool(name="keep", bufs=1))
-        psum = ctx.enter_context(tc.psum_pool(name="psum", bufs=8))
+        psum = ctx.enter_context(tc.psum_pool(name="psum", bufs=7))
+        spare = ctx.enter_context(tc.psum_pool(name="spare", bufs=1))
         ctx.enter_context(tc.manual_schedule())
+
+        zeros = keep.tile([P, N_TILE], BF16, name="zeros")
+        idle_bank = spare.tile([P, N_TILE], F32, name="idle_bank")
+
+        def keep_clock_up(count):
+            for unused in range(count):
+                nc.tensor.matmul(out=idle_bank[:], lhsT=zeros[:, 0:P], rhs=zeros[:], start=True, stop=True)
 
         ident = keep.tile([P, P], F32, name="ident")
         order = keep.tile([P, 8], F32, name="order")
@@ -88,6 +97,7 @@ def tile_quantlinear_kernel(tc, x, w_words, w_scales, out):
         make_identity(nc, ident[:])
         for m in range(ROW_TILES):
             nc.sync.dma_start(out=x_raw[m][:], in_=x[m])
+        nc.vector.memset(zeros[:], 0.0)
         zero_planes(0)
         nc.vector.tensor_copy(out=order[:, 0:1], in_=ident[:, 0:1])
         for s in range(1, len(PLANE_GROUPS)):
@@ -101,19 +111,21 @@ def tile_quantlinear_kernel(tc, x, w_words, w_scales, out):
             cols = slice(first * N_TILE // 2, (first + count) * N_TILE // 2)
             nc.sync.dma_start(out=w_chunk[c][:].bitcast(I32), in_=words_dram[:, :, cols])
 
-        banks = []
         for m in range(ROW_TILES):
+            keep_clock_up(IDLE_MATMULS[m])
             x_words = x_raw[m][:].bitcast(F32)
+            banks = []
             for g in range(PASSES):
                 xt = psum.tile([P, 2, P], F32, name="xt%d_%d" % (m, g), tag="bank")
                 for u in range(2):
                     nc.tensor.transpose(xt[:, u, :], x_words[:, 256 * g + u : 256 * (g + 1) : 2], ident[:])
                 banks.append(xt)
-        for m in range(ROW_TILES):
+            if m == ROW_TILES - 1:
+                keep_clock_up(IDLE_MATMULS[ROW_TILES])
             for h in range(2):
                 view = grouped[2 * m + h][:].bitcast(F32)
-                nc.vector.tensor_copy(out=view[:, 0], in_=banks[4 * m + 2 * h][:].rearrange("p u r -> p r u"))
-                nc.scalar.copy(out=view[:, 1], in_=banks[4 * m + 2 * h + 1][:].rearrange("p u r -> p r u"))
+                nc.vector.tensor_copy(out=view[:, 0], in_=banks[2 * h][:].rearrange("p u r -> p r u"))
+                nc.scalar.copy(out=view[:, 1], in_=banks[2 * h + 1][:].rearrange("p u r -> p r u"))
             for h in range(2):
                 i = 2 * m + h
                 nc.vector.quantize_mx(

@@ -18,11 +18,10 @@ N_TILE = 512
 COL_TILES = 11
 FLOPS = 2 * 256 * 2048 * 5632
 
-WORD_CHUNKS = ((1, 2), (3, 2), (5, 2), (7, 4))
-PLANE_GROUPS = ((0, 3), (3, 3), (6, 3), (9, 2))
-GATE_AFTER_TILE = ((2, 2), (3, 5))
+WORD_CHUNKS = ((1, 2), (3, 2), (5, 2), (7, 2), (9, 2))
+EARLY_CHUNKS = 3
+PLANE_GROUPS = ((0, 3), (3, 3), (6, 5))
 STORE_GROUPS = ((0, 3), (3, 3), (6, 2), (8, 2), (10, 1))
-IDLE_MATMULS = (7, 2, 2)
 
 
 def find(groups, j):
@@ -40,19 +39,12 @@ def tile_quantlinear_kernel(tc, x, w_words, w_scales, out):
 
     with ExitStack() as ctx:
         keep = ctx.enter_context(tc.tile_pool(name="keep", bufs=1))
-        psum = ctx.enter_context(tc.psum_pool(name="psum", bufs=7))
-        spare = ctx.enter_context(tc.psum_pool(name="spare", bufs=1))
+        psum = ctx.enter_context(tc.psum_pool(name="psum", bufs=8))
         ctx.enter_context(tc.manual_schedule())
-
-        zeros = keep.tile([P, N_TILE], BF16, name="zeros")
-        idle_bank = spare.tile([P, N_TILE], F32, name="idle_bank")
-
-        def keep_clock_up(count):
-            for unused in range(count):
-                nc.tensor.matmul(out=idle_bank[:], lhsT=zeros[:, 0:P], rhs=zeros[:], start=True, stop=True)
 
         ident = keep.tile([P, P], F32, name="ident")
         order = keep.tile([P, 8], F32, name="order")
+        order_words = keep.tile([P, 8], I32, name="order_words")
         x_raw = [keep.tile([P, 2048], BF16, name="x_raw%d" % m) for m in range(ROW_TILES)]
         grouped = [
             keep.tile([P, 2, P, 4], BF16, name="grouped%d" % i, align_bytes=64) for i in range(2 * ROW_TILES)
@@ -90,14 +82,19 @@ def tile_quantlinear_kernel(tc, x, w_words, w_scales, out):
                             in_=scales_i32[4 * b + r : 16 : 8, :, cols],
                         )
 
-        def let_go(s):
+        def load_words(c):
+            first, count = WORD_CHUNKS[c]
+            cols = slice(first * N_TILE // 2, (first + count) * N_TILE // 2)
+            nc.sync.dma_start(out=w_chunk[c][:].bitcast(I32), in_=words_dram[:, :, cols])
+
+        def let_go(s, landed):
+            nc.vector.tensor_copy(out=order_words[:, 0:1], in_=w_chunk[landed][:].bitcast(I32)[:, 0, 0:1])
             nc.vector.memset(w_plane[s][:].bitcast(I32)[:, 0, 0:1], 0)
             load_planes(s, True)
 
         make_identity(nc, ident[:])
         for m in range(ROW_TILES):
             nc.sync.dma_start(out=x_raw[m][:], in_=x[m])
-        nc.vector.memset(zeros[:], 0.0)
         zero_planes(0)
         nc.vector.tensor_copy(out=order[:, 0:1], in_=ident[:, 0:1])
         for s in range(1, len(PLANE_GROUPS)):
@@ -105,27 +102,24 @@ def tile_quantlinear_kernel(tc, x, w_words, w_scales, out):
         load_planes(0, False)
         for g in range(PASSES):
             nc.sync.dma_start(out=w_first[g][:].bitcast(I32), in_=words_dram[:, g, 0 : N_TILE // 2])
-        for c, (first, count) in enumerate(WORD_CHUNKS):
+        for c in range(EARLY_CHUNKS):
             if c == 1:
                 load_planes(1, False)
-            cols = slice(first * N_TILE // 2, (first + count) * N_TILE // 2)
-            nc.sync.dma_start(out=w_chunk[c][:].bitcast(I32), in_=words_dram[:, :, cols])
+            load_words(c)
 
+        banks = []
         for m in range(ROW_TILES):
-            keep_clock_up(IDLE_MATMULS[m])
             x_words = x_raw[m][:].bitcast(F32)
-            banks = []
             for g in range(PASSES):
                 xt = psum.tile([P, 2, P], F32, name="xt%d_%d" % (m, g), tag="bank")
                 for u in range(2):
                     nc.tensor.transpose(xt[:, u, :], x_words[:, 256 * g + u : 256 * (g + 1) : 2], ident[:])
                 banks.append(xt)
-            if m == ROW_TILES - 1:
-                keep_clock_up(IDLE_MATMULS[ROW_TILES])
+        for m in range(ROW_TILES):
             for h in range(2):
                 view = grouped[2 * m + h][:].bitcast(F32)
-                nc.vector.tensor_copy(out=view[:, 0], in_=banks[2 * h][:].rearrange("p u r -> p r u"))
-                nc.scalar.copy(out=view[:, 1], in_=banks[2 * h + 1][:].rearrange("p u r -> p r u"))
+                nc.vector.tensor_copy(out=view[:, 0], in_=banks[4 * m + 2 * h][:].rearrange("p u r -> p r u"))
+                nc.scalar.copy(out=view[:, 1], in_=banks[4 * m + 2 * h + 1][:].rearrange("p u r -> p r u"))
             for h in range(2):
                 i = 2 * m + h
                 nc.vector.quantize_mx(
@@ -159,9 +153,8 @@ def tile_quantlinear_kernel(tc, x, w_words, w_scales, out):
                 dst = staged[m][t][:, N_TILE * ti : N_TILE * (ti + 1)]
                 if m == 0:
                     nc.vector.tensor_copy(out=dst, in_=acc[:])
-                    for s_late, gate_tile in GATE_AFTER_TILE:
-                        if gate_tile == j:
-                            let_go(s_late)
+                    if j == 2:
+                        let_go(2, 1)
                 else:
                     nc.scalar.copy(out=dst, in_=acc[:])
             first, count = STORE_GROUPS[t]
@@ -170,3 +163,6 @@ def tile_quantlinear_kernel(tc, x, w_words, w_scales, out):
                     nc.sync.dma_start(
                         out=out[m, :, first * N_TILE : (first + count) * N_TILE], in_=staged[m][t][:]
                     )
+                if t == 0:
+                    for c in range(EARLY_CHUNKS, len(WORD_CHUNKS)):
+                        load_words(c)

@@ -18,10 +18,11 @@ N_TILE = 512
 COL_TILES = 11
 FLOPS = 2 * 256 * 2048 * 5632
 
-WORD_CHUNKS = ((1, 2), (3, 2), (5, 2), (7, 2), (9, 2))
-EARLY_CHUNKS = 3
-PLANE_GROUPS = ((0, 3), (3, 3), (6, 5))
+WORD_CHUNKS = ((1, 1), (2, 1), (3, 2), (5, 2), (7, 2), (9, 2))
+PLANE_GROUPS = ((0, 3), (3, 3), (6, 3), (9, 2))
+GATE_AFTER_TILE = ((2, 0), (3, 3))
 STORE_GROUPS = ((0, 3), (3, 3), (6, 2), (8, 2), (10, 1))
+IDLE_MATMULS = (7, 2, 2)
 
 
 def find(groups, j):
@@ -34,24 +35,30 @@ def find(groups, j):
 def tile_quantlinear_kernel(tc, x, w_words, w_scales, out):
     nc = tc.nc
     words_dram = w_words.bitcast(I32).rearrange("g p b -> p g b")
-    scales_i32 = w_scales.bitcast(I32).rearrange("g q b -> q g b")
     scales_f32 = w_scales.bitcast(F32).rearrange("g q b -> q g b")
 
     with ExitStack() as ctx:
         keep = ctx.enter_context(tc.tile_pool(name="keep", bufs=1))
-        psum = ctx.enter_context(tc.psum_pool(name="psum", bufs=8))
+        psum = ctx.enter_context(tc.psum_pool(name="psum", bufs=7))
+        spare = ctx.enter_context(tc.psum_pool(name="spare", bufs=1))
         ctx.enter_context(tc.manual_schedule())
+
+        zeros = keep.tile([P, N_TILE], BF16, name="zeros")
+        idle_bank = spare.tile([P, N_TILE], F32, name="idle_bank")
+
+        def keep_clock_up(count):
+            for unused in range(count):
+                nc.tensor.matmul(out=idle_bank[:], lhsT=zeros[:, 0:P], rhs=zeros[:], start=True, stop=True)
 
         ident = keep.tile([P, P], F32, name="ident")
         order = keep.tile([P, 8], F32, name="order")
-        order_words = keep.tile([P, 8], I32, name="order_words")
         x_raw = [keep.tile([P, 2048], BF16, name="x_raw%d" % m) for m in range(ROW_TILES)]
         grouped = [
             keep.tile([P, 2, P, 4], BF16, name="grouped%d" % i, align_bytes=64) for i in range(2 * ROW_TILES)
         ]
         x_codes = [keep.tile([P, 2 * P], U32, name="x_codes%d" % i, align_bytes=64) for i in range(2 * ROW_TILES)]
         x_plane = [keep.tile([P, 2 * P], U8, name="x_plane%d" % i, align_bytes=64) for i in range(2 * ROW_TILES)]
-        w_first = [keep.tile([P, 2 * N_TILE], U8, name="w_first%d" % g, align_bytes=64) for g in range(PASSES)]
+        w_first = [keep.tile([P, 2, 2 * N_TILE], U8, name="w_first%d" % h, align_bytes=64) for h in range(2)]
         w_chunk = [
             keep.tile([P, PASSES, 2 * N_TILE * count], U8, name="w_chunk%d" % c, align_bytes=64)
             for c, (first, count) in enumerate(WORD_CHUNKS)
@@ -71,55 +78,45 @@ def tile_quantlinear_kernel(tc, x, w_words, w_scales, out):
         def load_planes(s, software_queue):
             first, count = PLANE_GROUPS[s]
             cols = slice(first * N_TILE // 4, (first + count) * N_TILE // 4)
-            if software_queue:
-                for r in range(4):
-                    nc.gpsimd.dma_start(out=w_plane[s][:].bitcast(F32)[r:P:32, :, :], in_=scales_f32[r:16:4, :, cols])
-            else:
-                for b in range(2):
-                    for r in range(4):
-                        nc.sync.dma_start(
-                            out=w_plane[s][:].bitcast(I32)[32 * b + r : P : 64, :, :],
-                            in_=scales_i32[4 * b + r : 16 : 8, :, cols],
-                        )
+            queue = nc.gpsimd if software_queue else nc.scalar
+            for r in range(4):
+                queue.dma_start(out=w_plane[s][:].bitcast(F32)[r:P:32, :, :], in_=scales_f32[r:16:4, :, cols])
 
-        def load_words(c):
-            first, count = WORD_CHUNKS[c]
-            cols = slice(first * N_TILE // 2, (first + count) * N_TILE // 2)
-            nc.sync.dma_start(out=w_chunk[c][:].bitcast(I32), in_=words_dram[:, :, cols])
-
-        def let_go(s, landed):
-            nc.vector.tensor_copy(out=order_words[:, 0:1], in_=w_chunk[landed][:].bitcast(I32)[:, 0, 0:1])
+        def let_go(s):
             nc.vector.memset(w_plane[s][:].bitcast(I32)[:, 0, 0:1], 0)
             load_planes(s, True)
 
         make_identity(nc, ident[:])
+        zero_planes(0)
+        load_planes(0, False)
         for m in range(ROW_TILES):
             nc.sync.dma_start(out=x_raw[m][:], in_=x[m])
-        zero_planes(0)
+        nc.vector.memset(zeros[:], 0.0)
         nc.vector.tensor_copy(out=order[:, 0:1], in_=ident[:, 0:1])
         for s in range(1, len(PLANE_GROUPS)):
             zero_planes(s)
-        load_planes(0, False)
-        for g in range(PASSES):
-            nc.sync.dma_start(out=w_first[g][:].bitcast(I32), in_=words_dram[:, g, 0 : N_TILE // 2])
-        for c in range(EARLY_CHUNKS):
-            if c == 1:
-                load_planes(1, False)
-            load_words(c)
+        load_planes(1, True)
+        for h in range(2):
+            nc.sync.dma_start(out=w_first[h][:].bitcast(I32), in_=words_dram[:, 2 * h : 2 * h + 2, 0 : N_TILE // 2])
+        for c, (first, count) in enumerate(WORD_CHUNKS):
+            cols = slice(first * N_TILE // 2, (first + count) * N_TILE // 2)
+            nc.sync.dma_start(out=w_chunk[c][:].bitcast(I32), in_=words_dram[:, :, cols])
 
-        banks = []
         for m in range(ROW_TILES):
+            keep_clock_up(IDLE_MATMULS[m])
             x_words = x_raw[m][:].bitcast(F32)
+            banks = []
             for g in range(PASSES):
                 xt = psum.tile([P, 2, P], F32, name="xt%d_%d" % (m, g), tag="bank")
                 for u in range(2):
                     nc.tensor.transpose(xt[:, u, :], x_words[:, 256 * g + u : 256 * (g + 1) : 2], ident[:])
                 banks.append(xt)
-        for m in range(ROW_TILES):
+            if m == ROW_TILES - 1:
+                keep_clock_up(IDLE_MATMULS[ROW_TILES])
             for h in range(2):
                 view = grouped[2 * m + h][:].bitcast(F32)
-                nc.vector.tensor_copy(out=view[:, 0], in_=banks[4 * m + 2 * h][:].rearrange("p u r -> p r u"))
-                nc.scalar.copy(out=view[:, 1], in_=banks[4 * m + 2 * h + 1][:].rearrange("p u r -> p r u"))
+                nc.vector.tensor_copy(out=view[:, 0], in_=banks[2 * h][:].rearrange("p u r -> p r u"))
+                nc.scalar.copy(out=view[:, 1], in_=banks[2 * h + 1][:].rearrange("p u r -> p r u"))
             for h in range(2):
                 i = 2 * m + h
                 nc.vector.quantize_mx(
@@ -137,7 +134,7 @@ def tile_quantlinear_kernel(tc, x, w_words, w_scales, out):
                     i = 2 * m + g // 2
                     tok = slice(P * (g % 2), P * (g % 2 + 1))
                     if j == 0:
-                        words = w_first[g][:]
+                        words = w_first[g // 2][:, g % 2, :]
                     else:
                         c, ci = find(WORD_CHUNKS, j)
                         words = w_chunk[c][:, g, 2 * N_TILE * ci : 2 * N_TILE * (ci + 1)]
@@ -153,8 +150,9 @@ def tile_quantlinear_kernel(tc, x, w_words, w_scales, out):
                 dst = staged[m][t][:, N_TILE * ti : N_TILE * (ti + 1)]
                 if m == 0:
                     nc.vector.tensor_copy(out=dst, in_=acc[:])
-                    if j == 2:
-                        let_go(2, 1)
+                    for s_late, gate_tile in GATE_AFTER_TILE:
+                        if gate_tile == j:
+                            let_go(s_late)
                 else:
                     nc.scalar.copy(out=dst, in_=acc[:])
             first, count = STORE_GROUPS[t]
@@ -163,6 +161,3 @@ def tile_quantlinear_kernel(tc, x, w_words, w_scales, out):
                     nc.sync.dma_start(
                         out=out[m, :, first * N_TILE : (first + count) * N_TILE], in_=staged[m][t][:]
                     )
-                if t == 0:
-                    for c in range(EARLY_CHUNKS, len(WORD_CHUNKS)):
-                        load_words(c)

@@ -18,11 +18,10 @@ N_TILE = 512
 COL_TILES = 11
 FLOPS = 2 * 256 * 2048 * 5632
 
-WORD_CHUNKS = ((1, 1), (2, 1), (3, 2), (5, 2), (7, 2), (9, 2))
+WORD_CHUNKS = ((1, 2), (3, 2), (5, 2), (7, 4))
 PLANE_GROUPS = ((0, 3), (3, 3), (6, 3), (9, 2))
-GATE_AFTER_TILE = ((2, 0), (3, 3))
+GATE_AFTER_TILE = ((2, 2), (3, 5))
 STORE_GROUPS = ((0, 3), (3, 3), (6, 2), (8, 2), (10, 1))
-IDLE_MATMULS = (7, 2, 2)
 
 
 def find(groups, j):
@@ -35,20 +34,13 @@ def find(groups, j):
 def tile_quantlinear_kernel(tc, x, w_words, w_scales, out):
     nc = tc.nc
     words_dram = w_words.bitcast(I32).rearrange("g p b -> p g b")
+    scales_i32 = w_scales.bitcast(I32).rearrange("g q b -> q g b")
     scales_f32 = w_scales.bitcast(F32).rearrange("g q b -> q g b")
 
     with ExitStack() as ctx:
         keep = ctx.enter_context(tc.tile_pool(name="keep", bufs=1))
-        psum = ctx.enter_context(tc.psum_pool(name="psum", bufs=7))
-        spare = ctx.enter_context(tc.psum_pool(name="spare", bufs=1))
+        psum = ctx.enter_context(tc.psum_pool(name="psum", bufs=8))
         ctx.enter_context(tc.manual_schedule())
-
-        zeros = keep.tile([P, N_TILE], BF16, name="zeros")
-        idle_bank = spare.tile([P, N_TILE], F32, name="idle_bank")
-
-        def keep_clock_up(count):
-            for unused in range(count):
-                nc.tensor.matmul(out=idle_bank[:], lhsT=zeros[:, 0:P], rhs=zeros[:], start=True, stop=True)
 
         ident = keep.tile([P, P], F32, name="ident")
         order = keep.tile([P, 8], F32, name="order")
@@ -58,7 +50,7 @@ def tile_quantlinear_kernel(tc, x, w_words, w_scales, out):
         ]
         x_codes = [keep.tile([P, 2 * P], U32, name="x_codes%d" % i, align_bytes=64) for i in range(2 * ROW_TILES)]
         x_plane = [keep.tile([P, 2 * P], U8, name="x_plane%d" % i, align_bytes=64) for i in range(2 * ROW_TILES)]
-        w_first = [keep.tile([P, 2, 2 * N_TILE], U8, name="w_first%d" % h, align_bytes=64) for h in range(2)]
+        w_first = [keep.tile([P, 2 * N_TILE], U8, name="w_first%d" % g, align_bytes=64) for g in range(PASSES)]
         w_chunk = [
             keep.tile([P, PASSES, 2 * N_TILE * count], U8, name="w_chunk%d" % c, align_bytes=64)
             for c, (first, count) in enumerate(WORD_CHUNKS)
@@ -68,9 +60,15 @@ def tile_quantlinear_kernel(tc, x, w_words, w_scales, out):
             for s, (first, count) in enumerate(PLANE_GROUPS)
         ]
         staged = [
-            [keep.tile([P, N_TILE * count], F32, name="staged%d_%d" % (m, t)) for t, (first, count) in enumerate(STORE_GROUPS)]
+            [
+                keep.tile([P, N_TILE * count], F32, name="staged%d_%d" % (m, t))
+                for t, (first, count) in enumerate(STORE_GROUPS)
+                if m < ROW_TILES - 1 or t < len(STORE_GROUPS) - 1
+            ]
             for m in range(ROW_TILES)
         ]
+
+        staged_last = [keep.tile([P, P], F32, name="staged_last%d" % n) for n in range(N_TILE // P)]
 
         def zero_planes(s):
             nc.vector.memset(w_plane[s][:].bitcast(I32), 0)
@@ -78,45 +76,50 @@ def tile_quantlinear_kernel(tc, x, w_words, w_scales, out):
         def load_planes(s, software_queue):
             first, count = PLANE_GROUPS[s]
             cols = slice(first * N_TILE // 4, (first + count) * N_TILE // 4)
-            queue = nc.gpsimd if software_queue else nc.scalar
-            for r in range(4):
-                queue.dma_start(out=w_plane[s][:].bitcast(F32)[r:P:32, :, :], in_=scales_f32[r:16:4, :, cols])
+            if software_queue:
+                for r in range(4):
+                    nc.gpsimd.dma_start(out=w_plane[s][:].bitcast(F32)[r:P:32, :, :], in_=scales_f32[r:16:4, :, cols])
+            else:
+                for b in range(2):
+                    for r in range(4):
+                        nc.sync.dma_start(
+                            out=w_plane[s][:].bitcast(I32)[32 * b + r : P : 64, :, :],
+                            in_=scales_i32[4 * b + r : 16 : 8, :, cols],
+                        )
 
         def let_go(s):
             nc.vector.memset(w_plane[s][:].bitcast(I32)[:, 0, 0:1], 0)
             load_planes(s, True)
 
         make_identity(nc, ident[:])
-        zero_planes(0)
-        load_planes(0, False)
         for m in range(ROW_TILES):
             nc.sync.dma_start(out=x_raw[m][:], in_=x[m])
-        nc.vector.memset(zeros[:], 0.0)
+        zero_planes(0)
         nc.vector.tensor_copy(out=order[:, 0:1], in_=ident[:, 0:1])
         for s in range(1, len(PLANE_GROUPS)):
             zero_planes(s)
-        load_planes(1, True)
-        for h in range(2):
-            nc.sync.dma_start(out=w_first[h][:].bitcast(I32), in_=words_dram[:, 2 * h : 2 * h + 2, 0 : N_TILE // 2])
+        load_planes(0, False)
+        for g in range(PASSES):
+            nc.sync.dma_start(out=w_first[g][:].bitcast(I32), in_=words_dram[:, g, 0 : N_TILE // 2])
         for c, (first, count) in enumerate(WORD_CHUNKS):
+            if c == 1:
+                load_planes(1, False)
             cols = slice(first * N_TILE // 2, (first + count) * N_TILE // 2)
             nc.sync.dma_start(out=w_chunk[c][:].bitcast(I32), in_=words_dram[:, :, cols])
 
+        banks = []
         for m in range(ROW_TILES):
-            keep_clock_up(IDLE_MATMULS[m])
             x_words = x_raw[m][:].bitcast(F32)
-            banks = []
             for g in range(PASSES):
                 xt = psum.tile([P, 2, P], F32, name="xt%d_%d" % (m, g), tag="bank")
                 for u in range(2):
                     nc.tensor.transpose(xt[:, u, :], x_words[:, 256 * g + u : 256 * (g + 1) : 2], ident[:])
                 banks.append(xt)
-            if m == ROW_TILES - 1:
-                keep_clock_up(IDLE_MATMULS[ROW_TILES])
+        for m in range(ROW_TILES):
             for h in range(2):
                 view = grouped[2 * m + h][:].bitcast(F32)
-                nc.vector.tensor_copy(out=view[:, 0], in_=banks[2 * h][:].rearrange("p u r -> p r u"))
-                nc.scalar.copy(out=view[:, 1], in_=banks[2 * h + 1][:].rearrange("p u r -> p r u"))
+                nc.vector.tensor_copy(out=view[:, 0], in_=banks[4 * m + 2 * h][:].rearrange("p u r -> p r u"))
+                nc.scalar.copy(out=view[:, 1], in_=banks[4 * m + 2 * h + 1][:].rearrange("p u r -> p r u"))
             for h in range(2):
                 i = 2 * m + h
                 nc.vector.quantize_mx(
@@ -129,12 +132,14 @@ def tile_quantlinear_kernel(tc, x, w_words, w_scales, out):
             s, si = find(PLANE_GROUPS, j)
             t, ti = find(STORE_GROUPS, j)
             for m in range(ROW_TILES):
+                if j == COL_TILES - 1 and m == ROW_TILES - 1:
+                    break
                 acc = psum.tile([P, N_TILE], F32, name="acc%d_%d" % (m, j), tag="bank")
                 for g in range(PASSES):
                     i = 2 * m + g // 2
                     tok = slice(P * (g % 2), P * (g % 2 + 1))
                     if j == 0:
-                        words = w_first[g // 2][:, g % 2, :]
+                        words = w_first[g][:]
                     else:
                         c, ci = find(WORD_CHUNKS, j)
                         words = w_chunk[c][:, g, 2 * N_TILE * ci : 2 * N_TILE * (ci + 1)]
@@ -157,7 +162,31 @@ def tile_quantlinear_kernel(tc, x, w_words, w_scales, out):
                     nc.scalar.copy(out=dst, in_=acc[:])
             first, count = STORE_GROUPS[t]
             if ti == count - 1:
-                for m in range(ROW_TILES):
+                for m in range(ROW_TILES if j < COL_TILES - 1 else ROW_TILES - 1):
                     nc.sync.dma_start(
                         out=out[m, :, first * N_TILE : (first + count) * N_TILE], in_=staged[m][t][:]
                     )
+
+        j = COL_TILES - 1
+        m = ROW_TILES - 1
+        c, ci = find(WORD_CHUNKS, j)
+        s, si = find(PLANE_GROUPS, j)
+        for n in range(N_TILE // P):
+            acc = psum.tile([P, P], F32, name="acc_last%d" % n, tag="bank")
+            for g in range(PASSES):
+                i = 2 * m + g // 2
+                tok = slice(P * (g % 2), P * (g % 2 + 1))
+                nc.tensor.matmul_mx(
+                    out=acc[:],
+                    lhsT=x_codes[i][:, tok].bitcast(FP8X4),
+                    lhsT_scale=x_plane[i][:, tok],
+                    rhs=w_chunk[c][:, g, 2 * (N_TILE * ci + P * n) : 2 * (N_TILE * ci + P * (n + 1))].bitcast(FP4X4),
+                    rhs_scale=w_plane[s][:, g, N_TILE * si + P * n : N_TILE * si + P * (n + 1)],
+                    start=(g == 0),
+                    stop=(g == PASSES - 1),
+                )
+            if n % 2 == 0:
+                nc.vector.tensor_copy(out=staged_last[n][:], in_=acc[:])
+            else:
+                nc.scalar.copy(out=staged_last[n][:], in_=acc[:])
+            nc.sync.dma_start(out=out[m, :, N_TILE * j + P * n : N_TILE * j + P * (n + 1)], in_=staged_last[n][:])

@@ -20,8 +20,8 @@ FLOPS = 2 * 256 * 2048 * 5632
 
 WORD_CHUNKS = ((1, 2), (3, 2), (5, 2), (7, 4))
 PLANE_GROUPS = ((0, 3), (3, 3), (6, 3), (9, 2))
-GATE_AFTER_TILE = ((2, 2), (3, 5))
-STORE_GROUPS = ((0, 3), (3, 3), (6, 2), (8, 2), (10, 1))
+GATE_AFTER_TILE = ((2, 1), (3, 4))
+STORE_GROUPS = ((0, 4), (4, 4), (8, 2), (10, 1))
 
 
 def find(groups, j):
@@ -60,15 +60,9 @@ def tile_quantlinear_kernel(tc, x, w_words, w_scales, out):
             for s, (first, count) in enumerate(PLANE_GROUPS)
         ]
         staged = [
-            [
-                keep.tile([P, N_TILE * count], F32, name="staged%d_%d" % (m, t))
-                for t, (first, count) in enumerate(STORE_GROUPS)
-                if m < ROW_TILES - 1 or t < len(STORE_GROUPS) - 1
-            ]
+            [keep.tile([P, N_TILE * count], F32, name="staged%d_%d" % (m, t)) for t, (first, count) in enumerate(STORE_GROUPS)]
             for m in range(ROW_TILES)
         ]
-
-        staged_last = [keep.tile([P, P], F32, name="staged_last%d" % n) for n in range(N_TILE // P)]
 
         def zero_planes(s):
             nc.vector.memset(w_plane[s][:].bitcast(I32), 0)
@@ -132,8 +126,6 @@ def tile_quantlinear_kernel(tc, x, w_words, w_scales, out):
             s, si = find(PLANE_GROUPS, j)
             t, ti = find(STORE_GROUPS, j)
             for m in range(ROW_TILES):
-                if j == COL_TILES - 1 and m == ROW_TILES - 1:
-                    break
                 acc = psum.tile([P, N_TILE], F32, name="acc%d_%d" % (m, j), tag="bank")
                 for g in range(PASSES):
                     i = 2 * m + g // 2
@@ -162,31 +154,7 @@ def tile_quantlinear_kernel(tc, x, w_words, w_scales, out):
                     nc.scalar.copy(out=dst, in_=acc[:])
             first, count = STORE_GROUPS[t]
             if ti == count - 1:
-                for m in range(ROW_TILES if j < COL_TILES - 1 else ROW_TILES - 1):
+                for m in range(ROW_TILES):
                     nc.sync.dma_start(
                         out=out[m, :, first * N_TILE : (first + count) * N_TILE], in_=staged[m][t][:]
                     )
-
-        j = COL_TILES - 1
-        m = ROW_TILES - 1
-        c, ci = find(WORD_CHUNKS, j)
-        s, si = find(PLANE_GROUPS, j)
-        for n in range(N_TILE // P):
-            acc = psum.tile([P, P], F32, name="acc_last%d" % n, tag="bank")
-            for g in range(PASSES):
-                i = 2 * m + g // 2
-                tok = slice(P * (g % 2), P * (g % 2 + 1))
-                nc.tensor.matmul_mx(
-                    out=acc[:],
-                    lhsT=x_codes[i][:, tok].bitcast(FP8X4),
-                    lhsT_scale=x_plane[i][:, tok],
-                    rhs=w_chunk[c][:, g, 2 * (N_TILE * ci + P * n) : 2 * (N_TILE * ci + P * (n + 1))].bitcast(FP4X4),
-                    rhs_scale=w_plane[s][:, g, N_TILE * si + P * n : N_TILE * si + P * (n + 1)],
-                    start=(g == 0),
-                    stop=(g == PASSES - 1),
-                )
-            if n % 2 == 0:
-                nc.vector.tensor_copy(out=staged_last[n][:], in_=acc[:])
-            else:
-                nc.scalar.copy(out=staged_last[n][:], in_=acc[:])
-            nc.sync.dma_start(out=out[m, :, N_TILE * j + P * n : N_TILE * j + P * (n + 1)], in_=staged_last[n][:])

from contextlib import ExitStack

import concourse.mybir as mybir
from concourse.masks import make_identity

F32 = mybir.dt.float32
BF16 = mybir.dt.bfloat16
I32 = mybir.dt.int32
U8 = mybir.dt.uint8
U32 = mybir.dt.uint32
FP8X4 = mybir.dt.float8_e4m3fn_x4
FP4X4 = mybir.dt.float4_e2m1fn_x4

P = 128
ROW_TILES = 2
PASSES = 4
N_TILE = 512
COL_TILES = 11
FLOPS = 2 * 256 * 2048 * 5632

WORD_CHUNKS = ((1, 2), (3, 2), (5, 2), (7, 4))
PLANE_GROUPS = ((0, 3), (3, 3), (6, 3), (9, 2))
GATE_AFTER_TILE = ((2, 1), (3, 4))
STORE_GROUPS = ((0, 4), (4, 4), (8, 2), (10, 1))


def find(groups, j):
    for idx, (first, count) in enumerate(groups):
        if first <= j < first + count:
            return idx, j - first
    raise ValueError("column tile outside the groups")


def tile_quantlinear_kernel(tc, x, w_words, w_scales, out):
    nc = tc.nc
    words_dram = w_words.bitcast(I32).rearrange("g p b -> p g b")
    scales_i32 = w_scales.bitcast(I32).rearrange("g q b -> q g b")
    scales_f32 = w_scales.bitcast(F32).rearrange("g q b -> q g b")

    with ExitStack() as ctx:
        keep = ctx.enter_context(tc.tile_pool(name="keep", bufs=1))
        psum = ctx.enter_context(tc.psum_pool(name="psum", bufs=8))
        ctx.enter_context(tc.manual_schedule())

        ident = keep.tile([P, P], F32, name="ident")
        order = keep.tile([P, 8], F32, name="order")
        x_raw = [keep.tile([P, 2048], BF16, name="x_raw%d" % m) for m in range(ROW_TILES)]
        grouped = [
            keep.tile([P, 2, P, 4], BF16, name="grouped%d" % i, align_bytes=64) for i in range(2 * ROW_TILES)
        ]
        x_codes = [keep.tile([P, 2 * P], U32, name="x_codes%d" % i, align_bytes=64) for i in range(2 * ROW_TILES)]
        x_plane = [keep.tile([P, 2 * P], U8, name="x_plane%d" % i, align_bytes=64) for i in range(2 * ROW_TILES)]
        w_first = [keep.tile([P, 2 * N_TILE], U8, name="w_first%d" % g, align_bytes=64) for g in range(PASSES)]
        w_chunk = [
            keep.tile([P, PASSES, 2 * N_TILE * count], U8, name="w_chunk%d" % c, align_bytes=64)
            for c, (first, count) in enumerate(WORD_CHUNKS)
        ]
        w_plane = [
            keep.tile([P, PASSES, N_TILE * count], U8, name="w_plane%d" % s, align_bytes=64)
            for s, (first, count) in enumerate(PLANE_GROUPS)
        ]
        staged = [
            [keep.tile([P, N_TILE * count], F32, name="staged%d_%d" % (m, t)) for t, (first, count) in enumerate(STORE_GROUPS)]
            for m in range(ROW_TILES)
        ]

        def zero_planes(s):
            nc.vector.memset(w_plane[s][:].bitcast(I32), 0)

        def load_planes(s, software_queue):
            first, count = PLANE_GROUPS[s]
            cols = slice(first * N_TILE // 4, (first + count) * N_TILE // 4)
            if software_queue:
                for r in range(4):
                    nc.gpsimd.dma_start(out=w_plane[s][:].bitcast(F32)[r:P:32, :, :], in_=scales_f32[r:16:4, :, cols])
            else:
                for b in range(2):
                    for r in range(4):
                        nc.sync.dma_start(
                            out=w_plane[s][:].bitcast(I32)[32 * b + r : P : 64, :, :],
                            in_=scales_i32[4 * b + r : 16 : 8, :, cols],
                        )

        def let_go(s):
            nc.vector.memset(w_plane[s][:].bitcast(I32)[:, 0, 0:1], 0)
            load_planes(s, True)

        make_identity(nc, ident[:])
        for m in range(ROW_TILES):
            nc.sync.dma_start(out=x_raw[m][:], in_=x[m])
        zero_planes(0)
        nc.vector.tensor_copy(out=order[:, 0:1], in_=ident[:, 0:1])
        for s in range(1, len(PLANE_GROUPS)):
            zero_planes(s)
        load_planes(0, False)
        for g in range(PASSES):
            nc.sync.dma_start(out=w_first[g][:].bitcast(I32), in_=words_dram[:, g, 0 : N_TILE // 2])
        for c, (first, count) in enumerate(WORD_CHUNKS):
            if c == 1:
                load_planes(1, False)
            cols = slice(first * N_TILE // 2, (first + count) * N_TILE // 2)
            nc.sync.dma_start(out=w_chunk[c][:].bitcast(I32), in_=words_dram[:, :, cols])

        banks = []
        for m in range(ROW_TILES):
            x_words = x_raw[m][:].bitcast(F32)
            for g in range(PASSES):
                xt = psum.tile([P, 2, P], F32, name="xt%d_%d" % (m, g), tag="bank")
                for u in range(2):
                    nc.tensor.transpose(xt[:, u, :], x_words[:, 256 * g + u : 256 * (g + 1) : 2], ident[:])
                banks.append(xt)
        for m in range(ROW_TILES):
            for h in range(2):
                view = grouped[2 * m + h][:].bitcast(F32)
                nc.vector.tensor_copy(out=view[:, 0], in_=banks[4 * m + 2 * h][:].rearrange("p u r -> p r u"))
                nc.scalar.copy(out=view[:, 1], in_=banks[4 * m + 2 * h + 1][:].rearrange("p u r -> p r u"))
            for h in range(2):
                i = 2 * m + h
                nc.vector.quantize_mx(
                    out=x_codes[i][:].bitcast(FP8X4),
                    scales=x_plane[i][:],
                    in_=grouped[i][:].rearrange("p g r t -> p (g r t)"),
                )

        for j in range(COL_TILES):
            s, si = find(PLANE_GROUPS, j)
            t, ti = find(STORE_GROUPS, j)
            for m in range(ROW_TILES):
                acc = psum.tile([P, N_TILE], F32, name="acc%d_%d" % (m, j), tag="bank")
                for g in range(PASSES):
                    i = 2 * m + g // 2
                    tok = slice(P * (g % 2), P * (g % 2 + 1))
                    if j == 0:
                        words = w_first[g][:]
                    else:
                        c, ci = find(WORD_CHUNKS, j)
                        words = w_chunk[c][:, g, 2 * N_TILE * ci : 2 * N_TILE * (ci + 1)]
                    nc.tensor.matmul_mx(
                        out=acc[:],
                        lhsT=x_codes[i][:, tok].bitcast(FP8X4),
                        lhsT_scale=x_plane[i][:, tok],
                        rhs=words.bitcast(FP4X4),
                        rhs_scale=w_plane[s][:, g, N_TILE * si : N_TILE * (si + 1)],
                        start=(g == 0),
                        stop=(g == PASSES - 1),
                    )
                dst = staged[m][t][:, N_TILE * ti : N_TILE * (ti + 1)]
                if m == 0:
                    nc.vector.tensor_copy(out=dst, in_=acc[:])
                    for s_late, gate_tile in GATE_AFTER_TILE:
                        if gate_tile == j:
                            let_go(s_late)
                else:
                    nc.scalar.copy(out=dst, in_=acc[:])
            first, count = STORE_GROUPS[t]
            if ti == count - 1:
                for m in range(ROW_TILES):
                    nc.sync.dma_start(
                        out=out[m, :, first * N_TILE : (first + count) * N_TILE], in_=staged[m][t][:]
                    )
